import numpy as np
import ml_dtypes

BF16 = ml_dtypes.bfloat16


def bf(x):
    return np.asarray(x, np.float32).astype(BF16)


def f32(x):
    return np.asarray(x, np.float32)


def f64(x):
    return np.asarray(x).astype(np.float64)


def striped(idx):
    return np.tile(idx.reshape(-1, 16).T, (8, 1))


S, D, E, K, M, N = 1024, 128, 128, 256, 512, 1024


def relu(v):
    return np.maximum(v, 0.0)


def setup_inputs():
    return {"table": bf(np.random.standard_normal((S, D))), "w": bf(np.random.standard_normal((D, M)) / np.sqrt(D + D)), "eb1": f32(0.2 * np.random.standard_normal((E, 1))), "wmid": bf(np.random.standard_normal((E, K)) / np.sqrt(E + E)), "nb1": f32(0.2 * np.random.standard_normal((K, 1))), "nw2": bf(np.random.standard_normal((K, D)) / np.sqrt(K)), "nb2": f32(0.2 * np.random.standard_normal((D, 1))), "offs": striped(np.random.permutation(np.tile(np.arange(S), 2))[:N])}


def reference(table, w, eb1, wmid, nb1, nw2, nb2, offs):
    idx = offs[:16].T.reshape(-1)
    h = f64(table)[idx].T
    proj = f64(w).T @ h
    p = proj[:E]
    qb = proj[E:E + E] + f64(eb1)
    r = proj[E + E:]
    u = np.zeros_like(qb)
    u[:, 1:] += relu(p[:, :-1] + qb[:, 1:])
    u[:, :-1] += relu(p[:, 1:] + qb[:, :-1])
    v = relu(r + f64(wmid).T @ u + f64(nb1))
    return h + f64(nw2).T @ v + f64(nb2)

@@ -1,0 +1,128 @@
+import concourse.mybir as mybir
+from concourse.masks import make_identity
+
+P = 128
+S = 1024
+N = 1024
+K_BLOCKS = 2
+PIECE = 512
+PIECES = N // PIECE
+PIECE_COLUMNS = PIECE // 16
+HALVES = 2
+BLOCKS = S // (HALVES * P)
+
+FLOPS = 2 * N * (P * 4 * P + P * K_BLOCKS * P + K_BLOCKS * P * P)
+
+BF16, F32, U16 = mybir.dt.bfloat16, mybir.dt.float32, mybir.dt.uint16
+ADD, MAX = mybir.AluOpType.add, mybir.AluOpType.max
+IDENTITY, RELU = mybir.ActivationFunctionType.Identity, mybir.ActivationFunctionType.Relu
+
+
+def tile_graphnetlayer_kernel(tc, table, w, eb1, wmid, nb1, nw2, nb2, offs, out):
+    nc = tc.nc
+    with (
+        tc.tile_pool(name="held", bufs=1) as held,
+        tc.tile_pool(name="work", bufs=PIECES) as work,
+        tc.psum_pool(name="banks", bufs=8) as banks,
+    ):
+        halves_dram = table.rearrange("(h a p) d -> h p a d", h=HALVES, p=P)
+        rows = [held.tile([P, BLOCKS, P], BF16, name=f"rows{h}") for h in range(HALVES)]
+        nc.sync.dma_start(rows[0][:], halves_dram[0])
+        nc.scalar.dma_start(rows[1][:], halves_dram[1])
+        offsets = held.tile([P, N // 16], U16, name="offsets")
+        nc.sync.dma_start(offsets[:], offs)
+        w_sb = held.tile([P, 4 * P], BF16, name="w_sb")
+        nc.scalar.dma_start(w_sb[:], w)
+        wmid_sb = held.tile([P, K_BLOCKS * P], BF16, name="wmid_sb")
+        nc.sync.dma_start(wmid_sb[:], wmid)
+        nw2_sb = held.tile([P, K_BLOCKS, P], BF16, name="nw2_sb")
+        nc.scalar.dma_start(nw2_sb[:], nw2.rearrange("(b p) d -> p b d", p=P))
+        eb1_sb = held.tile([P, 1], F32, name="eb1_sb")
+        nc.gpsimd.dma_start(eb1_sb[:], eb1)
+        nb1_sb = [held.tile([P, 1], F32, name=f"nb1_sb{b}") for b in range(K_BLOCKS)]
+        for b in range(K_BLOCKS):
+            nc.gpsimd.dma_start(nb1_sb[b][:], nb1[b * P : (b + 1) * P, :])
+        nb2_sb = held.tile([P, 1], F32, name="nb2_sb")
+        nc.gpsimd.dma_start(nb2_sb[:], nb2)
+
+        identity = held.tile([P, P], BF16, name="identity")
+        make_identity(nc, identity[:])
+
+        nodes = held.tile([P, S], BF16, name="nodes")
+        for h in range(HALVES):
+            flipped = banks.tile([P, BLOCKS * P], BF16, tag="bank", name=f"flipped{h}")
+            for a in range(BLOCKS):
+                nc.tensor.transpose(flipped[:, a * P : (a + 1) * P], rows[h][:, a, :], identity[:])
+            half = nodes[:, h * BLOCKS * P : (h + 1) * BLOCKS * P]
+            if h == 0:
+                nc.vector.tensor_copy(half, flipped[:])
+            else:
+                nc.scalar.copy(half, flipped[:])
+
+        def walk(c):
+            return nodes[:].indirect(offsets[:, c * PIECE_COLUMNS : (c + 1) * PIECE_COLUMNS])
+
+        def bank(name):
+            return banks.tile([P, PIECE], F32, tag="bank", name=name)
+
+        p_ps = [bank(f"p_ps{c}") for c in range(PIECES)]
+        for c in range(PIECES):
+            nc.tensor.matmul(p_ps[c][:], w_sb[:, 0:P], walk(c), start=True, stop=True)
+        pb = held.tile([P, N], F32, name="pb")
+        for c in range(PIECES):
+            nc.scalar.activation(pb[:, c * PIECE : (c + 1) * PIECE], p_ps[c][:], IDENTITY, bias=eb1_sb[:])
+        q_ps = [bank(f"q_ps{c}") for c in range(PIECES)]
+        for c in range(PIECES):
+            nc.tensor.matmul(q_ps[c][:], w_sb[:, P : 2 * P], walk(c), start=True, stop=True)
+        hidden_ps = [[bank(f"hidden_ps{c}_{b}") for b in range(K_BLOCKS)] for c in range(PIECES)]
+        for c in range(PIECES):
+            for b in range(K_BLOCKS):
+                r_weights = w_sb[:, (2 + b) * P : (3 + b) * P]
+                nc.tensor.matmul(hidden_ps[c][b][:], r_weights, walk(c), start=True, stop=False)
+        out_ps = [bank(f"out_ps{c}") for c in range(PIECES)]
+        for c in range(PIECES):
+            nc.tensor.matmul(out_ps[c][:], identity[:], walk(c), start=True, stop=False)
+
+        u = []
+        for c in range(PIECES):
+            j0 = c * PIECE
+            first = 1 if c == 0 else 0
+            last = PIECE - 1 if c == PIECES - 1 else PIECE
+            before = work.tile([P, PIECE], F32, name="before")
+            after = work.tile([P, PIECE], F32, name="after")
+            if first > 0:
+                nc.vector.memset(before[:, 0:first], 0.0)
+            if last < PIECE:
+                nc.vector.memset(after[:, last:PIECE], 0.0)
+            nc.vector.tensor_tensor(
+                before[:, first:PIECE], q_ps[c][:, first:PIECE], pb[:, j0 + first - 1 : j0 + PIECE - 1], ADD
+            )
+            nc.vector.tensor_tensor(after[:, 0:last], q_ps[c][:, 0:last], pb[:, j0 + 1 : j0 + last + 1], ADD)
+            before_relu = work.tile([P, PIECE], F32, name="before_relu")
+            nc.scalar.activation(before_relu[:], before[:], RELU)
+            u_c = work.tile([P, PIECE], BF16, name="u_c")
+            nc.vector.scalar_tensor_tensor(u_c[:], after[:], 0.0, before_relu[:], op0=MAX, op1=ADD)
+            u.append(u_c)
+
+        v = []
+        for c in range(PIECES):
+            for b in range(K_BLOCKS):
+                nc.tensor.matmul(
+                    hidden_ps[c][b][:], wmid_sb[:, b * P : (b + 1) * P], u[c][:], start=False, stop=True
+                )
+            v_c = [work.tile([P, PIECE], BF16, name=f"v_c{b}") for b in range(K_BLOCKS)]
+            nc.scalar.activation(v_c[0][:], hidden_ps[c][0][:], RELU, bias=nb1_sb[0][:])
+            nc.vector.tensor_scalar(v_c[1][:], hidden_ps[c][1][:], nb1_sb[1][:], 0.0, op0=ADD, op1=MAX)
+            v.append(v_c)
+
+        for c in range(PIECES):
+            for b in range(K_BLOCKS):
+                nc.tensor.matmul(
+                    out_ps[c][:], nw2_sb[:, b, :], v[c][b][:], start=False, stop=(b == K_BLOCKS - 1)
+                )
+            result = work.tile([P, PIECE], F32, name="result")
+            if c % 2 == 0:
+                nc.scalar.activation(result[:], out_ps[c][:], IDENTITY, bias=nb2_sb[:])
+            else:
+                nc.vector.tensor_scalar(result[:], out_ps[c][:], nb2_sb[:], None, op0=ADD)
+            nc.sync.dma_start(out[:, c * PIECE : (c + 1) * PIECE], result[:])

@@ -8,8 +8,9 @@ K_BLOCKS = 2
 PIECE = 512
 PIECES = N // PIECE
 PIECE_COLUMNS = PIECE // 16
-HALVES = 2
-BLOCKS = S // (HALVES * P)
+PARTS = 4
+BLOCKS = S // (PARTS * P)
+WARM_MATMULS = 4
 
 FLOPS = 2 * N * (P * 4 * P + P * K_BLOCKS * P + K_BLOCKS * P * P)
 
@@ -25,45 +26,52 @@ def tile_graphnetlayer_kernel(tc, table, w, eb1, wmid, nb1, nw2, nb2, offs, out)
         tc.tile_pool(name="work", bufs=PIECES) as work,
         tc.psum_pool(name="banks", bufs=8) as banks,
     ):
-        halves_dram = table.rearrange("(h a p) d -> h p a d", h=HALVES, p=P)
-        rows = [held.tile([P, BLOCKS, P], BF16, name=f"rows{h}") for h in range(HALVES)]
-        nc.sync.dma_start(rows[0][:], halves_dram[0])
-        nc.scalar.dma_start(rows[1][:], halves_dram[1])
+        identity = held.tile([P, P], BF16, name="identity")
+        make_identity(nc, identity[:])
+
+        parts_dram = table.rearrange("(h a p) d -> h p a d", h=PARTS, p=P)
+        rows = [held.tile([P, BLOCKS, P], BF16, name=f"rows{h}") for h in range(PARTS)]
+        for h in range(PARTS):
+            queue = nc.sync if h % 2 == 0 else nc.scalar
+            queue.dma_start(rows[h][:], parts_dram[h])
         offsets = held.tile([P, N // 16], U16, name="offsets")
         nc.sync.dma_start(offsets[:], offs)
         w_sb = held.tile([P, 4 * P], BF16, name="w_sb")
         nc.scalar.dma_start(w_sb[:], w)
+        eb1_sb = held.tile([P, 1], F32, name="eb1_sb")
+        nc.sync.dma_start(eb1_sb[:], eb1)
         wmid_sb = held.tile([P, K_BLOCKS * P], BF16, name="wmid_sb")
         nc.sync.dma_start(wmid_sb[:], wmid)
         nw2_sb = held.tile([P, K_BLOCKS, P], BF16, name="nw2_sb")
-        nc.scalar.dma_start(nw2_sb[:], nw2.rearrange("(b p) d -> p b d", p=P))
-        eb1_sb = held.tile([P, 1], F32, name="eb1_sb")
-        nc.gpsimd.dma_start(eb1_sb[:], eb1)
+        nc.sync.dma_start(nw2_sb[:], nw2.rearrange("(b p) d -> p b d", p=P))
         nb1_sb = [held.tile([P, 1], F32, name=f"nb1_sb{b}") for b in range(K_BLOCKS)]
         for b in range(K_BLOCKS):
-            nc.gpsimd.dma_start(nb1_sb[b][:], nb1[b * P : (b + 1) * P, :])
+            nc.sync.dma_start(nb1_sb[b][:], nb1[b * P : (b + 1) * P, :])
         nb2_sb = held.tile([P, 1], F32, name="nb2_sb")
-        nc.gpsimd.dma_start(nb2_sb[:], nb2)
-
-        identity = held.tile([P, P], BF16, name="identity")
-        make_identity(nc, identity[:])
-
-        nodes = held.tile([P, S], BF16, name="nodes")
-        for h in range(HALVES):
-            flipped = banks.tile([P, BLOCKS * P], BF16, tag="bank", name=f"flipped{h}")
-            for a in range(BLOCKS):
-                nc.tensor.transpose(flipped[:, a * P : (a + 1) * P], rows[h][:, a, :], identity[:])
-            half = nodes[:, h * BLOCKS * P : (h + 1) * BLOCKS * P]
-            if h == 0:
-                nc.vector.tensor_copy(half, flipped[:])
-            else:
-                nc.scalar.copy(half, flipped[:])
-
-        def walk(c):
-            return nodes[:].indirect(offsets[:, c * PIECE_COLUMNS : (c + 1) * PIECE_COLUMNS])
+        nc.sync.dma_start(nb2_sb[:], nb2)
 
         def bank(name):
             return banks.tile([P, PIECE], F32, tag="bank", name=name)
+
+        zeros = held.tile([P, PIECE], BF16, name="zeros")
+        nc.vector.memset(zeros[:], 0.0)
+        warm_ps = bank("warm_ps")
+        for i in range(WARM_MATMULS):
+            nc.tensor.matmul(warm_ps[:], zeros[:, 0:P], zeros[:], start=True, stop=True)
+
+        nodes = held.tile([P, S], BF16, name="nodes")
+        for h in range(PARTS):
+            flipped = banks.tile([P, BLOCKS * P], BF16, tag="bank", name=f"flipped{h}")
+            for a in range(BLOCKS):
+                nc.tensor.transpose(flipped[:, a * P : (a + 1) * P], rows[h][:, a, :], identity[:])
+            part = nodes[:, h * BLOCKS * P : (h + 1) * BLOCKS * P]
+            if h % 2 == 0:
+                nc.vector.tensor_copy(part, flipped[:])
+            else:
+                nc.scalar.copy(part, flipped[:])
+
+        def walk(c):
+            return nodes[:].indirect(offsets[:, c * PIECE_COLUMNS : (c + 1) * PIECE_COLUMNS])
 
         p_ps = [bank(f"p_ps{c}") for c in range(PIECES)]
         for c in range(PIECES):

@@ -10,7 +10,7 @@ PIECES = N // PIECE
 PIECE_COLUMNS = PIECE // 16
 PARTS = 4
 BLOCKS = S // (PARTS * P)
-WARM_MATMULS = 4
+WARM_MATMULS = 2
 
 FLOPS = 2 * N * (P * 4 * P + P * K_BLOCKS * P + K_BLOCKS * P * P)
 
@@ -91,25 +91,29 @@ def tile_graphnetlayer_kernel(tc, table, w, eb1, wmid, nb1, nw2, nb2, offs, out)
         for c in range(PIECES):
             nc.tensor.matmul(out_ps[c][:], identity[:], walk(c), start=True, stop=False)
 
-        u = []
+        before_relu, after = [], []
         for c in range(PIECES):
             j0 = c * PIECE
             first = 1 if c == 0 else 0
             last = PIECE - 1 if c == PIECES - 1 else PIECE
-            before = work.tile([P, PIECE], F32, name="before")
-            after = work.tile([P, PIECE], F32, name="after")
+            before_c = work.tile([P, PIECE], F32, name="before_c")
+            after_c = work.tile([P, PIECE], F32, name="after_c")
             if first > 0:
-                nc.vector.memset(before[:, 0:first], 0.0)
+                nc.vector.memset(before_c[:, 0:first], 0.0)
             if last < PIECE:
-                nc.vector.memset(after[:, last:PIECE], 0.0)
+                nc.vector.memset(after_c[:, last:PIECE], 0.0)
             nc.vector.tensor_tensor(
-                before[:, first:PIECE], q_ps[c][:, first:PIECE], pb[:, j0 + first - 1 : j0 + PIECE - 1], ADD
+                before_c[:, first:PIECE], q_ps[c][:, first:PIECE], pb[:, j0 + first - 1 : j0 + PIECE - 1], ADD
             )
-            nc.vector.tensor_tensor(after[:, 0:last], q_ps[c][:, 0:last], pb[:, j0 + 1 : j0 + last + 1], ADD)
-            before_relu = work.tile([P, PIECE], F32, name="before_relu")
-            nc.scalar.activation(before_relu[:], before[:], RELU)
+            nc.vector.tensor_tensor(after_c[:, 0:last], q_ps[c][:, 0:last], pb[:, j0 + 1 : j0 + last + 1], ADD)
+            before_relu_c = work.tile([P, PIECE], F32, name="before_relu_c")
+            nc.scalar.activation(before_relu_c[:], before_c[:], RELU)
+            before_relu.append(before_relu_c)
+            after.append(after_c)
+        u = []
+        for c in range(PIECES):
             u_c = work.tile([P, PIECE], BF16, name="u_c")
-            nc.vector.scalar_tensor_tensor(u_c[:], after[:], 0.0, before_relu[:], op0=MAX, op1=ADD)
+            nc.vector.scalar_tensor_tensor(u_c[:], after[c][:], 0.0, before_relu[c][:], op0=MAX, op1=ADD)
             u.append(u_c)
 
         v = []

@@ -10,7 +10,6 @@ PIECES = N // PIECE
 PIECE_COLUMNS = PIECE // 16
 PARTS = 4
 BLOCKS = S // (PARTS * P)
-WARM_MATMULS = 2
 
 FLOPS = 2 * N * (P * 4 * P + P * K_BLOCKS * P + K_BLOCKS * P * P)
 
@@ -52,12 +51,6 @@ def tile_graphnetlayer_kernel(tc, table, w, eb1, wmid, nb1, nw2, nb2, offs, out)
 
         def bank(name):
             return banks.tile([P, PIECE], F32, tag="bank", name=name)
-
-        zeros = held.tile([P, PIECE], BF16, name="zeros")
-        nc.vector.memset(zeros[:], 0.0)
-        warm_ps = bank("warm_ps")
-        for i in range(WARM_MATMULS):
-            nc.tensor.matmul(warm_ps[:], zeros[:, 0:P], zeros[:], start=True, stop=True)
 
         nodes = held.tile([P, S], BF16, name="nodes")
         for h in range(PARTS):

@@ -7,9 +7,10 @@ N = 1024
 K_BLOCKS = 2
 PIECE = 512
 PIECES = N // PIECE
-PIECE_COLUMNS = PIECE // 16
+CHUNKS = ((0, PIECE), (PIECE, PIECE // 2), (PIECE + PIECE // 2, PIECE // 2))
 PARTS = 4
 BLOCKS = S // (PARTS * P)
+WARM_MATMULS = 2
 
 FLOPS = 2 * N * (P * 4 * P + P * K_BLOCKS * P + K_BLOCKS * P * P)
 
@@ -22,7 +23,7 @@ def tile_graphnetlayer_kernel(tc, table, w, eb1, wmid, nb1, nw2, nb2, offs, out)
     nc = tc.nc
     with (
         tc.tile_pool(name="held", bufs=1) as held,
-        tc.tile_pool(name="work", bufs=PIECES) as work,
+        tc.tile_pool(name="work", bufs=len(CHUNKS)) as work,
         tc.psum_pool(name="banks", bufs=8) as banks,
     ):
         identity = held.tile([P, P], BF16, name="identity")
@@ -52,6 +53,12 @@ def tile_graphnetlayer_kernel(tc, table, w, eb1, wmid, nb1, nw2, nb2, offs, out)
         def bank(name):
             return banks.tile([P, PIECE], F32, tag="bank", name=name)
 
+        zeros = held.tile([P, PIECE], BF16, name="zeros")
+        nc.vector.memset(zeros[:], 0.0)
+        warm_ps = bank("warm_ps")
+        for i in range(WARM_MATMULS):
+            nc.tensor.matmul(warm_ps[:], zeros[:, 0:P], zeros[:], start=True, stop=True)
+
         nodes = held.tile([P, S], BF16, name="nodes")
         for h in range(PARTS):
             flipped = banks.tile([P, BLOCKS * P], BF16, tag="bank", name=f"flipped{h}")
@@ -63,26 +70,23 @@ def tile_graphnetlayer_kernel(tc, table, w, eb1, wmid, nb1, nw2, nb2, offs, out)
             else:
                 nc.scalar.copy(part, flipped[:])
 
-        def walk(c):
-            return nodes[:].indirect(offsets[:, c * PIECE_COLUMNS : (c + 1) * PIECE_COLUMNS])
+        def walk(j0, steps):
+            return nodes[:].indirect(offsets[:, j0 // 16 : (j0 + steps) // 16])
 
         p_ps = [bank(f"p_ps{c}") for c in range(PIECES)]
         for c in range(PIECES):
-            nc.tensor.matmul(p_ps[c][:], w_sb[:, 0:P], walk(c), start=True, stop=True)
+            nc.tensor.matmul(p_ps[c][:], w_sb[:, 0:P], walk(c * PIECE, PIECE), start=True, stop=True)
         pb = held.tile([P, N], F32, name="pb")
         for c in range(PIECES):
             nc.scalar.activation(pb[:, c * PIECE : (c + 1) * PIECE], p_ps[c][:], IDENTITY, bias=eb1_sb[:])
         q_ps = [bank(f"q_ps{c}") for c in range(PIECES)]
         for c in range(PIECES):
-            nc.tensor.matmul(q_ps[c][:], w_sb[:, P : 2 * P], walk(c), start=True, stop=True)
+            nc.tensor.matmul(q_ps[c][:], w_sb[:, P : 2 * P], walk(c * PIECE, PIECE), start=True, stop=True)
         hidden_ps = [[bank(f"hidden_ps{c}_{b}") for b in range(K_BLOCKS)] for c in range(PIECES)]
         for c in range(PIECES):
             for b in range(K_BLOCKS):
                 r_weights = w_sb[:, (2 + b) * P : (3 + b) * P]
-                nc.tensor.matmul(hidden_ps[c][b][:], r_weights, walk(c), start=True, stop=False)
-        out_ps = [bank(f"out_ps{c}") for c in range(PIECES)]
-        for c in range(PIECES):
-            nc.tensor.matmul(out_ps[c][:], identity[:], walk(c), start=True, stop=False)
+                nc.tensor.matmul(hidden_ps[c][b][:], r_weights, walk(c * PIECE, PIECE), start=True, stop=False)
 
         before_relu, after = [], []
         for c in range(PIECES):
@@ -109,25 +113,35 @@ def tile_graphnetlayer_kernel(tc, table, w, eb1, wmid, nb1, nw2, nb2, offs, out)
             nc.vector.scalar_tensor_tensor(u_c[:], after[c][:], 0.0, before_relu[c][:], op0=MAX, op1=ADD)
             u.append(u_c)
 
-        v = []
+        out_ps = []
+        for j0, steps in CHUNKS:
+            out_ps_k = banks.tile([P, steps], F32, tag="bank", name="out_ps_k")
+            nc.tensor.matmul(out_ps_k[:], identity[:], walk(j0, steps), start=True, stop=False)
+            out_ps.append(out_ps_k)
+
         for c in range(PIECES):
             for b in range(K_BLOCKS):
                 nc.tensor.matmul(
                     hidden_ps[c][b][:], wmid_sb[:, b * P : (b + 1) * P], u[c][:], start=False, stop=True
                 )
-            v_c = [work.tile([P, PIECE], BF16, name=f"v_c{b}") for b in range(K_BLOCKS)]
-            nc.scalar.activation(v_c[0][:], hidden_ps[c][0][:], RELU, bias=nb1_sb[0][:])
-            nc.vector.tensor_scalar(v_c[1][:], hidden_ps[c][1][:], nb1_sb[1][:], 0.0, op0=ADD, op1=MAX)
-            v.append(v_c)
+        v = []
+        for j0, steps in CHUNKS:
+            c, local = divmod(j0, PIECE)
+            v_k = [work.tile([P, steps], BF16, name=f"v_k{b}") for b in range(K_BLOCKS)]
+            nc.scalar.activation(v_k[0][:], hidden_ps[c][0][:, local : local + steps], RELU, bias=nb1_sb[0][:])
+            nc.vector.tensor_scalar(
+                v_k[1][:], hidden_ps[c][1][:, local : local + steps], nb1_sb[1][:], 0.0, op0=ADD, op1=MAX
+            )
+            v.append(v_k)
 
-        for c in range(PIECES):
+        for k, (j0, steps) in enumerate(CHUNKS):
             for b in range(K_BLOCKS):
                 nc.tensor.matmul(
-                    out_ps[c][:], nw2_sb[:, b, :], v[c][b][:], start=False, stop=(b == K_BLOCKS - 1)
+                    out_ps[k][:], nw2_sb[:, b, :], v[k][b][:], start=False, stop=(b == K_BLOCKS - 1)
                 )
-            result = work.tile([P, PIECE], F32, name="result")
-            if c % 2 == 0:
-                nc.scalar.activation(result[:], out_ps[c][:], IDENTITY, bias=nb2_sb[:])
+            result = work.tile([P, steps], F32, name="result")
+            if k % 2 == 0:
+                nc.scalar.activation(result[:], out_ps[k][:], IDENTITY, bias=nb2_sb[:])
             else:
-                nc.vector.tensor_scalar(result[:], out_ps[c][:], nb2_sb[:], None, op0=ADD)
-            nc.sync.dma_start(out[:, c * PIECE : (c + 1) * PIECE], result[:])
+                nc.vector.tensor_scalar(result[:], out_ps[k][:], nb2_sb[:], None, op0=ADD)
+            nc.sync.dma_start(out[:, j0 : j0 + steps], result[:])

@@ -7,7 +7,7 @@ N = 1024
 K_BLOCKS = 2
 PIECE = 512
 PIECES = N // PIECE
-CHUNKS = ((0, PIECE), (PIECE, PIECE // 2), (PIECE + PIECE // 2, PIECE // 2))
+CHUNKS = tuple((k * (PIECE // 2), PIECE // 2) for k in range(2 * PIECES))
 PARTS = 4
 BLOCKS = S // (PARTS * P)
 WARM_MATMULS = 2

@@ -65,10 +65,7 @@ def tile_graphnetlayer_kernel(tc, table, w, eb1, wmid, nb1, nw2, nb2, offs, out)
             for a in range(BLOCKS):
                 nc.tensor.transpose(flipped[:, a * P : (a + 1) * P], rows[h][:, a, :], identity[:])
             part = nodes[:, h * BLOCKS * P : (h + 1) * BLOCKS * P]
-            if h % 2 == 0:
-                nc.vector.tensor_copy(part, flipped[:])
-            else:
-                nc.scalar.copy(part, flipped[:])
+            nc.vector.tensor_copy(part, flipped[:])
 
         def walk(j0, steps):
             return nodes[:].indirect(offsets[:, j0 // 16 : (j0 + steps) // 16])

import concourse.mybir as mybir
from concourse.masks import make_identity

P = 128
S = 1024
N = 1024
K_BLOCKS = 2
PIECE = 512
PIECES = N // PIECE
CHUNKS = tuple((k * (PIECE // 2), PIECE // 2) for k in range(2 * PIECES))
PARTS = 4
BLOCKS = S // (PARTS * P)
WARM_MATMULS = 2

FLOPS = 2 * N * (P * 4 * P + P * K_BLOCKS * P + K_BLOCKS * P * P)

BF16, F32, U16 = mybir.dt.bfloat16, mybir.dt.float32, mybir.dt.uint16
ADD, MAX = mybir.AluOpType.add, mybir.AluOpType.max
IDENTITY, RELU = mybir.ActivationFunctionType.Identity, mybir.ActivationFunctionType.Relu


def tile_graphnetlayer_kernel(tc, table, w, eb1, wmid, nb1, nw2, nb2, offs, out):
    nc = tc.nc
    with (
        tc.tile_pool(name="held", bufs=1) as held,
        tc.tile_pool(name="work", bufs=len(CHUNKS)) as work,
        tc.psum_pool(name="banks", bufs=8) as banks,
    ):
        identity = held.tile([P, P], BF16, name="identity")
        make_identity(nc, identity[:])

        parts_dram = table.rearrange("(h a p) d -> h p a d", h=PARTS, p=P)
        rows = [held.tile([P, BLOCKS, P], BF16, name=f"rows{h}") for h in range(PARTS)]
        for h in range(PARTS):
            queue = nc.sync if h % 2 == 0 else nc.scalar
            queue.dma_start(rows[h][:], parts_dram[h])
        offsets = held.tile([P, N // 16], U16, name="offsets")
        nc.sync.dma_start(offsets[:], offs)
        w_sb = held.tile([P, 4 * P], BF16, name="w_sb")
        nc.scalar.dma_start(w_sb[:], w)
        eb1_sb = held.tile([P, 1], F32, name="eb1_sb")
        nc.sync.dma_start(eb1_sb[:], eb1)
        wmid_sb = held.tile([P, K_BLOCKS * P], BF16, name="wmid_sb")
        nc.sync.dma_start(wmid_sb[:], wmid)
        nw2_sb = held.tile([P, K_BLOCKS, P], BF16, name="nw2_sb")
        nc.sync.dma_start(nw2_sb[:], nw2.rearrange("(b p) d -> p b d", p=P))
        nb1_sb = [held.tile([P, 1], F32, name=f"nb1_sb{b}") for b in range(K_BLOCKS)]
        for b in range(K_BLOCKS):
            nc.sync.dma_start(nb1_sb[b][:], nb1[b * P : (b + 1) * P, :])
        nb2_sb = held.tile([P, 1], F32, name="nb2_sb")
        nc.sync.dma_start(nb2_sb[:], nb2)

        def bank(name):
            return banks.tile([P, PIECE], F32, tag="bank", name=name)

        zeros = held.tile([P, PIECE], BF16, name="zeros")
        nc.vector.memset(zeros[:], 0.0)
        warm_ps = bank("warm_ps")
        for i in range(WARM_MATMULS):
            nc.tensor.matmul(warm_ps[:], zeros[:, 0:P], zeros[:], start=True, stop=True)

        nodes = held.tile([P, S], BF16, name="nodes")
        for h in range(PARTS):
            flipped = banks.tile([P, BLOCKS * P], BF16, tag="bank", name=f"flipped{h}")
            for a in range(BLOCKS):
                nc.tensor.transpose(flipped[:, a * P : (a + 1) * P], rows[h][:, a, :], identity[:])
            part = nodes[:, h * BLOCKS * P : (h + 1) * BLOCKS * P]
            nc.vector.tensor_copy(part, flipped[:])

        def walk(j0, steps):
            return nodes[:].indirect(offsets[:, j0 // 16 : (j0 + steps) // 16])

        p_ps = [bank(f"p_ps{c}") for c in range(PIECES)]
        for c in range(PIECES):
            nc.tensor.matmul(p_ps[c][:], w_sb[:, 0:P], walk(c * PIECE, PIECE), start=True, stop=True)
        pb = held.tile([P, N], F32, name="pb")
        for c in range(PIECES):
            nc.scalar.activation(pb[:, c * PIECE : (c + 1) * PIECE], p_ps[c][:], IDENTITY, bias=eb1_sb[:])
        q_ps = [bank(f"q_ps{c}") for c in range(PIECES)]
        for c in range(PIECES):
            nc.tensor.matmul(q_ps[c][:], w_sb[:, P : 2 * P], walk(c * PIECE, PIECE), start=True, stop=True)
        hidden_ps = [[bank(f"hidden_ps{c}_{b}") for b in range(K_BLOCKS)] for c in range(PIECES)]
        for c in range(PIECES):
            for b in range(K_BLOCKS):
                r_weights = w_sb[:, (2 + b) * P : (3 + b) * P]
                nc.tensor.matmul(hidden_ps[c][b][:], r_weights, walk(c * PIECE, PIECE), start=True, stop=False)

        before_relu, after = [], []
        for c in range(PIECES):
            j0 = c * PIECE
            first = 1 if c == 0 else 0
            last = PIECE - 1 if c == PIECES - 1 else PIECE
            before_c = work.tile([P, PIECE], F32, name="before_c")
            after_c = work.tile([P, PIECE], F32, name="after_c")
            if first > 0:
                nc.vector.memset(before_c[:, 0:first], 0.0)
            if last < PIECE:
                nc.vector.memset(after_c[:, last:PIECE], 0.0)
            nc.vector.tensor_tensor(
                before_c[:, first:PIECE], q_ps[c][:, first:PIECE], pb[:, j0 + first - 1 : j0 + PIECE - 1], ADD
            )
            nc.vector.tensor_tensor(after_c[:, 0:last], q_ps[c][:, 0:last], pb[:, j0 + 1 : j0 + last + 1], ADD)
            before_relu_c = work.tile([P, PIECE], F32, name="before_relu_c")
            nc.scalar.activation(before_relu_c[:], before_c[:], RELU)
            before_relu.append(before_relu_c)
            after.append(after_c)
        u = []
        for c in range(PIECES):
            u_c = work.tile([P, PIECE], BF16, name="u_c")
            nc.vector.scalar_tensor_tensor(u_c[:], after[c][:], 0.0, before_relu[c][:], op0=MAX, op1=ADD)
            u.append(u_c)

        out_ps = []
        for j0, steps in CHUNKS:
            out_ps_k = banks.tile([P, steps], F32, tag="bank", name="out_ps_k")
            nc.tensor.matmul(out_ps_k[:], identity[:], walk(j0, steps), start=True, stop=False)
            out_ps.append(out_ps_k)

        for c in range(PIECES):
            for b in range(K_BLOCKS):
                nc.tensor.matmul(
                    hidden_ps[c][b][:], wmid_sb[:, b * P : (b + 1) * P], u[c][:], start=False, stop=True
                )
        v = []
        for j0, steps in CHUNKS:
            c, local = divmod(j0, PIECE)
            v_k = [work.tile([P, steps], BF16, name=f"v_k{b}") for b in range(K_BLOCKS)]
            nc.scalar.activation(v_k[0][:], hidden_ps[c][0][:, local : local + steps], RELU, bias=nb1_sb[0][:])
            nc.vector.tensor_scalar(
                v_k[1][:], hidden_ps[c][1][:, local : local + steps], nb1_sb[1][:], 0.0, op0=ADD, op1=MAX
            )
            v.append(v_k)

        for k, (j0, steps) in enumerate(CHUNKS):
            for b in range(K_BLOCKS):
                nc.tensor.matmul(
                    out_ps[k][:], nw2_sb[:, b, :], v[k][b][:], start=False, stop=(b == K_BLOCKS - 1)
                )
            result = work.tile([P, steps], F32, name="result")
            if k % 2 == 0:
                nc.scalar.activation(result[:], out_ps[k][:], IDENTITY, bias=nb2_sb[:])
            else:
                nc.vector.tensor_scalar(result[:], out_ps[k][:], nb2_sb[:], None, op0=ADD)
            nc.sync.dma_start(out[:, j0 : j0 + steps], result[:])
